import numpy as np
import ml_dtypes


def mxq(x, axis, fmt="e4m3"):
    dtype, down = {"e4m3": (ml_dtypes.float8_e4m3fn, 7), "e5m2": (ml_dtypes.float8_e5m2, 14)}[fmt]
    v = np.moveaxis(np.asarray(x, np.float32).astype(ml_dtypes.bfloat16).astype(np.float64), axis, -1)
    blocks = v.reshape(v.shape[:-1] + (-1, 32))
    amax = np.abs(blocks).max(-1, keepdims=True)
    byte = np.maximum(np.where(amax > 0, np.frexp(amax)[1] - 1 + 127, 0) - down, 1)
    scale = np.exp2(byte - 127.0)
    codes = (blocks / scale).astype(np.float32).astype(dtype).astype(np.float64)
    return np.moveaxis((codes * scale).reshape(v.shape), -1, axis)


WIDE = False


def mx_kscale(k):
    if not WIDE:
        return np.ones(k)
    levels = np.array([10, -10, 5, -5, 0])
    a = np.random.permutation(np.resize(levels, k // 512 * 4)).reshape(k // 512, 4)
    idx = np.arange(k)
    return np.exp2(a[idx // 512, idx % 128 // 32])


BF16 = ml_dtypes.bfloat16


def bf(x):
    return np.asarray(x, np.float32).astype(BF16)


def f64(x):
    return np.asarray(x).astype(np.float64)


E2M1 = np.array([0.0, 0.5, 1.0, 1.5, 2.0, 3.0, 4.0, 6.0, -0.0, -0.5, -1.0, -1.5, -2.0, -3.0, -4.0, -6.0])


def pack_weight(w, fmt):
    k, n = w.shape
    w = f64(bf(w)).reshape(k // 32, 32, n)
    amax = np.abs(w).max(1)
    if fmt == "e4m3":
        byte = np.frexp(amax)[1] - 1 + 127 - 7
    else:
        mant, ex = np.frexp(amax / 6.0)
        byte = np.where(mant > 0.5, ex, ex - 1) + 127
    byte = np.clip(np.where(amax > 0, byte, 1), 1, 254)
    scaled = (w * np.exp2(127.0 - byte)[:, None, :]).reshape(k, n).astype(np.float32)
    by_word = np.ascontiguousarray(scaled.reshape(k // 512, 128, 4, n).transpose(0, 1, 3, 2))
    if fmt == "e4m3":
        words = by_word.astype(ml_dtypes.float8_e4m3fn).view(np.uint8)
    else:
        c = by_word.astype(ml_dtypes.float4_e2m1fn).view(np.uint8) & 0xF
        words = c[..., 0::2] | (c[..., 1::2] << 4)
    return np.ascontiguousarray(words), np.ascontiguousarray(byte.astype(np.uint8).reshape(k // 512, 16, n))


def unpack_weight(words, scales, fmt):
    g, p, n, _ = words.shape
    if fmt == "e4m3":
        vals = np.ascontiguousarray(words).view(ml_dtypes.float8_e4m3fn).astype(np.float64)
    else:
        nib = np.empty((g, p, n, 4), np.uint8)
        nib[..., 0::2] = words & 0xF
        nib[..., 1::2] = words >> 4
        vals = E2M1[nib]
    vals = vals * np.repeat(np.exp2(scales.astype(np.float64) - 127.0), 8, axis=1)[..., None]
    return vals.transpose(0, 1, 3, 2).reshape(g * 512, n)


B, S, E, H, D = 1, 128, 8192, 16, 128
ROPE_BASE = 10000.0
HALF = D // 2
FMT = "e4m3"


def rope_interleaved(t):
    inv_freq = 1.0 / (ROPE_BASE ** (np.arange(HALF) * 2.0 / D))
    ang = np.arange(S)[:, None] * inv_freq[None, :]
    cos = np.cos(ang)[None, :, None, :]
    sin = np.sin(ang)[None, :, None, :]
    t0 = t[..., 0::2]
    t1 = t[..., 1::2]
    out = np.stack([t0 * cos - t1 * sin, t1 * cos + t0 * sin], axis=-1)
    return out.reshape(B, S, H, D)


def setup_inputs():
    s = mx_kscale(E)
    x = bf(np.random.standard_normal((B, S, E)) * s)
    Wq_words, Wq_scales = pack_weight(np.random.standard_normal((E, H * D)) / np.sqrt(E) / s[:, None], FMT)
    Wk_words, Wk_scales = pack_weight(np.random.standard_normal((E, H * D)) / np.sqrt(E) / s[:, None], FMT)
    return {"x": x,
            "Wq_words": Wq_words, "Wq_scales": Wq_scales,
            "Wk_words": Wk_words, "Wk_scales": Wk_scales}


def reference(x, Wq_words, Wq_scales, Wk_words, Wk_scales):
    xq = mxq(f64(x), 2, "e4m3")
    q = (xq @ unpack_weight(Wq_words, Wq_scales, FMT)).reshape(B, S, H, D)
    k = (xq @ unpack_weight(Wk_words, Wk_scales, FMT)).reshape(B, S, H, D)
    q = rope_interleaved(q)
    k = rope_interleaved(k)
    return q.transpose(0, 2, 1, 3), k.transpose(0, 2, 1, 3)

@@ -1,0 +1,236 @@
+import math
+
+import concourse.mybir as mybir
+from concourse.masks import make_identity
+
+F32 = mybir.dt.float32
+BF16 = mybir.dt.bfloat16
+I32 = mybir.dt.int32
+U32 = mybir.dt.uint32
+U8 = mybir.dt.uint8
+FP8X4 = mybir.dt.float8_e4m3fn_x4
+SIN = mybir.ActivationFunctionType.Sin
+
+P = 128
+PACK = 4
+K_PASS = P * PACK
+FEATURES = 8192
+GROUPS = FEATURES // K_PASS
+HEADS = 16
+HEAD_DIM = 128
+HALF = HEAD_DIM // 2
+N_OUT = HEADS * HEAD_DIM
+N_TILE = 512
+BANKS = N_OUT // N_TILE
+HEADS_PER_BANK = N_TILE // HEAD_DIM
+ROPE_BASE = 10000.0
+ROUND_MAGIC = 1.5 * 2.0**23
+
+PLANE_ROWS = 4
+PLANES_PER_SET = 4
+SETS = GROUPS // PLANES_PER_SET
+TAIL_GROUPS = 4
+W_BUFS = 12
+
+FLOPS = 2 * P * FEATURES * 2 * N_OUT
+
+
+def build_rope_tables(nc, consts):
+    position_int = consts.tile([P, 1], I32)
+    nc.gpsimd.iota(position_int[:], pattern=[[0, 1]], base=0, channel_multiplier=1)
+    position = consts.tile([P, 1], F32)
+    nc.vector.tensor_copy(out=position[:], in_=position_int[:])
+    position_turns = consts.tile([P, 1], F32)
+    nc.vector.tensor_scalar_mul(out=position_turns[:], in0=position[:], scalar1=1.0 / (2.0 * math.pi))
+
+    frequency = consts.tile([P, HALF], F32)
+    nc.vector.memset(frequency[:, 0:1], 1.0)
+    width = 1
+    while width < HALF:
+        nc.vector.tensor_scalar_mul(
+            out=frequency[:, width : 2 * width],
+            in0=frequency[:, 0:width],
+            scalar1=ROPE_BASE ** (-2.0 * width / HEAD_DIM),
+        )
+        width *= 2
+
+    turns = consts.tile([P, 2, HALF], F32)
+    nc.vector.tensor_scalar_mul(out=turns[:, 0, :], in0=frequency[:], scalar1=position_turns[:, 0:1])
+    nc.vector.tensor_scalar_add(out=turns[:, 1, :], in0=turns[:, 0, :], scalar1=0.25)
+
+    shifted = consts.tile([P, 2, HALF], F32)
+    nc.vector.tensor_scalar_add(out=shifted[:], in0=turns[:], scalar1=ROUND_MAGIC)
+    whole = consts.tile([P, 2, HALF], F32)
+    nc.vector.tensor_scalar_sub(out=whole[:], in0=shifted[:], scalar1=ROUND_MAGIC)
+    part = consts.tile([P, 2, HALF], F32)
+    nc.vector.tensor_sub(out=part[:], in0=turns[:], in1=whole[:])
+
+    cos_pairs = consts.tile([P, HALF, 2], F32)
+    nc.scalar.activation(
+        out=cos_pairs[:],
+        in_=part[:, 1, :].unsqueeze(2).to_broadcast([P, HALF, 2]),
+        func=SIN,
+        scale=2.0 * math.pi,
+    )
+    sin_planes = consts.tile([P, 2, HALF], F32)
+    nc.scalar.activation(out=sin_planes[:, 0, :], in_=part[:, 0, :], func=SIN, scale=-2.0 * math.pi)
+    nc.scalar.activation(out=sin_planes[:, 1, :], in_=part[:, 0, :], func=SIN, scale=2.0 * math.pi)
+    return cos_pairs, sin_planes
+
+
+def quantise_x(nc, consts, psum, x):
+    identity = consts.tile([P, P], F32)
+    make_identity(nc, identity[:])
+
+    x_sb = consts.tile([P, FEATURES], BF16)
+    load_cols = FEATURES // 4
+    for piece in range(4):
+        cols = slice(piece * load_cols, (piece + 1) * load_cols)
+        nc.sync.dma_start(out=x_sb[:, cols], in_=x[0, :, cols])
+
+    x_words = x_sb[:].bitcast(F32)
+    words_per_pass = K_PASS // 2
+    grouped = consts.tile([P, GROUPS * K_PASS], BF16, align_bytes=64)
+    grouped_words = grouped[:].bitcast(F32)
+    x_codes = consts.tile([P, GROUPS * P], U32, align_bytes=64)
+    x_scales = consts.tile([P, GROUPS * P], U8, align_bytes=64)
+
+    passes_per_bank = 2
+    banks_per_quantise = 2
+    for bank in range(GROUPS // passes_per_bank):
+        xt = psum.tile([P, 2 * passes_per_bank, P], F32, tag="bank%d" % bank, name="xt")
+        for c in range(passes_per_bank):
+            first_word = (bank * passes_per_bank + c) * words_per_pass
+            for u in range(2):
+                nc.tensor.transpose(
+                    xt[:, 2 * c + u, :],
+                    x_words[:, first_word + u : first_word + words_per_pass : 2],
+                    identity[:],
+                )
+        bank_words = slice(bank * N_TILE, (bank + 1) * N_TILE)
+        side_by_side = grouped_words[:, bank_words].rearrange("p (c r u) -> p c r u", c=passes_per_bank, u=2)
+        transposed = xt[:].rearrange("p (c u) r -> p c r u", u=2)
+        if bank % 2 == 0:
+            nc.vector.tensor_copy(out=side_by_side, in_=transposed)
+        else:
+            nc.scalar.copy(out=side_by_side, in_=transposed)
+            first_pass = (bank + 1 - banks_per_quantise) * passes_per_bank
+            last_pass = (bank + 1) * passes_per_bank
+            nc.vector.quantize_mx(
+                out=x_codes[:, first_pass * P : last_pass * P].bitcast(FP8X4),
+                scales=x_scales[:, first_pass * P : last_pass * P],
+                in_=grouped[:, first_pass * K_PASS : last_pass * K_PASS],
+            )
+    return x_codes, x_scales
+
+
+def load_scale_planes(nc, planes, scales):
+    for s in range(SETS):
+        groups = slice(s * PLANES_PER_SET, (s + 1) * PLANES_PER_SET)
+        for quadrant in range(4):
+            nc.sync.dma_start(
+                out=planes[32 * quadrant : 32 * quadrant + PLANES_PER_SET * PLANE_ROWS, s, :].bitcast(I32),
+                in_=scales[groups, PLANE_ROWS * quadrant : PLANE_ROWS * (quadrant + 1), :].bitcast(I32),
+            )
+
+
+def multiply(nc, acc, x_codes, x_scales, g, w_codes, planes, cols):
+    positions = slice(g * P, (g + 1) * P)
+    first_row = PLANE_ROWS * (g % PLANES_PER_SET)
+    nc.tensor.matmul_mx(
+        out=acc[:],
+        lhsT=x_codes[:, positions].bitcast(FP8X4),
+        lhsT_scale=x_scales[:, positions],
+        rhs=w_codes.bitcast(FP8X4),
+        rhs_scale=planes[first_row:P, g // PLANES_PER_SET, cols],
+        start=(g == 0),
+        stop=(g == GROUPS - 1),
+    )
+
+
+def rotate_and_store(nc, work, acc, cos_pairs, sin_planes, out_heads, queue):
+    by_head = "p (h j) -> p h j"
+    pairs = acc[:].rearrange("p (h i e) -> p h i e", h=HEADS_PER_BANK, e=2)
+    half_shape = [P, HEADS_PER_BANK, HALF]
+
+    direct = work.tile([P, N_TILE], F32)
+    nc.vector.tensor_mul(
+        out=direct[:].rearrange(by_head, h=HEADS_PER_BANK),
+        in0=acc[:].rearrange(by_head, h=HEADS_PER_BANK),
+        in1=cos_pairs[:].rearrange("p i e -> p (i e)").unsqueeze(1).to_broadcast([P, HEADS_PER_BANK, HEAD_DIM]),
+    )
+    cross = work.tile([P, 2, N_TILE // 2], F32)
+    for e in range(2):
+        nc.vector.tensor_mul(
+            out=cross[:, e, :].rearrange("p (h i) -> p h i", h=HEADS_PER_BANK),
+            in0=pairs[:, :, :, 1 - e],
+            in1=sin_planes[:, e, :].unsqueeze(1).to_broadcast(half_shape),
+        )
+    rotated = work.tile([P, N_TILE], F32)
+    nc.vector.tensor_add(
+        out=rotated[:].rearrange("p (n e) -> p n e", e=2),
+        in0=direct[:].rearrange("p (n e) -> p n e", e=2),
+        in1=cross[:].rearrange("p e n -> p n e"),
+    )
+    queue.dma_start(
+        out=out_heads.rearrange("h p j -> p h j"),
+        in_=rotated[:].rearrange(by_head, h=HEADS_PER_BANK),
+    )
+
+
+def tile_multiheadselfattention_pa_k_kernel(
+    tc, x, Wq_words, Wq_scales, Wk_words, Wk_scales, out_0, out_1
+):
+    nc = tc.nc
+    with tc.tile_pool(name="consts", bufs=1) as consts, tc.tile_pool(
+        name="weights", bufs=W_BUFS
+    ) as weights, tc.tile_pool(name="work", bufs=4) as work, tc.psum_pool(name="psum", bufs=1) as psum:
+        q_planes = consts.tile([P, SETS, N_OUT], U8, align_bytes=64)
+        k_planes = consts.tile([P, SETS, N_OUT], U8, align_bytes=64)
+        nc.vector.memset(q_planes[:].bitcast(I32), 0)
+        nc.vector.memset(k_planes[:].bitcast(I32), 0)
+
+        x_codes, x_scales = quantise_x(nc, consts, psum, x)
+        load_scale_planes(nc, q_planes, Wq_scales)
+        load_scale_planes(nc, k_planes, Wk_scales)
+        cos_pairs, sin_planes = build_rope_tables(nc, consts)
+
+        q_acc = [psum.tile([P, N_TILE], F32, tag="bank%d" % b, name="q_acc%d" % b) for b in range(BANKS)]
+        for g in range(GROUPS):
+            w_tile = weights.tile([P, N_OUT], U32, tag="w", name="wq", align_bytes=64)
+            nc.sync.dma_start(
+                out=w_tile[:].bitcast(I32), in_=Wq_words[g].rearrange("p n t -> p (n t)").bitcast(I32)
+            )
+            for b in range(BANKS):
+                cols = slice(b * N_TILE, (b + 1) * N_TILE)
+                multiply(nc, q_acc[b], x_codes, x_scales, g, w_tile[:, cols], q_planes, cols)
+        for b in range(BANKS):
+            heads = slice(b * HEADS_PER_BANK, (b + 1) * HEADS_PER_BANK)
+            rotate_and_store(nc, work, q_acc[b], cos_pairs, sin_planes, out_0[0, heads], nc.scalar)
+
+        k_acc = [
+            psum.tile([P, N_TILE], F32, tag="bank%d" % (BANKS + b), name="k_acc%d" % b) for b in range(BANKS)
+        ]
+        for g in range(GROUPS - TAIL_GROUPS):
+            w_tile = weights.tile([P, N_OUT], U32, tag="w", name="wk", align_bytes=64)
+            nc.sync.dma_start(
+                out=w_tile[:].bitcast(I32), in_=Wk_words[g].rearrange("p n t -> p (n t)").bitcast(I32)
+            )
+            for b in range(BANKS):
+                cols = slice(b * N_TILE, (b + 1) * N_TILE)
+                multiply(nc, k_acc[b], x_codes, x_scales, g, w_tile[:, cols], k_planes, cols)
+        for b in range(BANKS):
+            cols = slice(b * N_TILE, (b + 1) * N_TILE)
+            w_tile = weights.tile([P, TAIL_GROUPS, N_TILE], U32, tag="w", name="wk_tail", align_bytes=64)
+            nc.sync.dma_start(
+                out=w_tile[:].bitcast(I32),
+                in_=Wk_words[GROUPS - TAIL_GROUPS : GROUPS, :, cols, :]
+                .rearrange("g p n t -> p g (n t)")
+                .bitcast(I32),
+            )
+            for i in range(TAIL_GROUPS):
+                multiply(
+                    nc, k_acc[b], x_codes, x_scales, GROUPS - TAIL_GROUPS + i, w_tile[:, i, :], k_planes, cols
+                )
+            heads = slice(b * HEADS_PER_BANK, (b + 1) * HEADS_PER_BANK)
+            rotate_and_store(nc, work, k_acc[b], cos_pairs, sin_planes, out_1[0, heads], nc.sync)

@@ -128,9 +128,9 @@ def load_scale_planes(nc, planes, scales):
     for s in range(SETS):
         groups = slice(s * PLANES_PER_SET, (s + 1) * PLANES_PER_SET)
         for quadrant in range(4):
-            nc.sync.dma_start(
-                out=planes[32 * quadrant : 32 * quadrant + PLANES_PER_SET * PLANE_ROWS, s, :].bitcast(I32),
-                in_=scales[groups, PLANE_ROWS * quadrant : PLANE_ROWS * (quadrant + 1), :].bitcast(I32),
+            nc.gpsimd.dma_start(
+                out=planes[32 * quadrant : 32 * quadrant + PLANES_PER_SET * PLANE_ROWS, s, :].bitcast(F32),
+                in_=scales[groups, PLANE_ROWS * quadrant : PLANE_ROWS * (quadrant + 1), :].bitcast(F32),
             )
 
 

@@ -148,7 +148,7 @@ def multiply(nc, acc, x_codes, x_scales, g, w_codes, planes, cols):
     )
 
 
-def rotate_and_store(nc, work, acc, cos_pairs, sin_planes, out_heads, queue):
+def rotate(nc, work, results, acc, cos_pairs, sin_planes):
     by_head = "p (h j) -> p h j"
     pairs = acc[:].rearrange("p (h i e) -> p h i e", h=HEADS_PER_BANK, e=2)
     half_shape = [P, HEADS_PER_BANK, HALF]
@@ -166,15 +166,20 @@ def rotate_and_store(nc, work, acc, cos_pairs, sin_planes, out_heads, queue):
             in0=pairs[:, :, :, 1 - e],
             in1=sin_planes[:, e, :].unsqueeze(1).to_broadcast(half_shape),
         )
-    rotated = work.tile([P, N_TILE], F32)
+    rotated = results.tile([P, N_TILE], F32)
     nc.vector.tensor_add(
         out=rotated[:].rearrange("p (n e) -> p n e", e=2),
         in0=direct[:].rearrange("p (n e) -> p n e", e=2),
         in1=cross[:].rearrange("p e n -> p n e"),
     )
-    queue.dma_start(
-        out=out_heads.rearrange("h p j -> p h j"),
-        in_=rotated[:].rearrange(by_head, h=HEADS_PER_BANK),
+    return rotated
+
+
+def store(nc, rotated, out, b):
+    heads = slice(b * HEADS_PER_BANK, (b + 1) * HEADS_PER_BANK)
+    nc.sync.dma_start(
+        out=out[0, heads].rearrange("h p j -> p h j"),
+        in_=rotated[:].rearrange("p (h j) -> p h j", h=HEADS_PER_BANK),
     )
 
 
@@ -184,16 +189,19 @@ def tile_multiheadselfattention_pa_k_kernel(
     nc = tc.nc
     with tc.tile_pool(name="consts", bufs=1) as consts, tc.tile_pool(
         name="weights", bufs=W_BUFS
-    ) as weights, tc.tile_pool(name="work", bufs=4) as work, tc.psum_pool(name="psum", bufs=1) as psum:
+    ) as weights, tc.tile_pool(name="work", bufs=2) as work, tc.tile_pool(
+        name="results", bufs=2 * BANKS
+    ) as results, tc.psum_pool(name="psum", bufs=1) as psum, tc.manual_schedule():
+
         q_planes = consts.tile([P, SETS, N_OUT], U8, align_bytes=64)
         k_planes = consts.tile([P, SETS, N_OUT], U8, align_bytes=64)
         nc.vector.memset(q_planes[:].bitcast(I32), 0)
         nc.vector.memset(k_planes[:].bitcast(I32), 0)
 
+        cos_pairs, sin_planes = build_rope_tables(nc, consts)
         x_codes, x_scales = quantise_x(nc, consts, psum, x)
         load_scale_planes(nc, q_planes, Wq_scales)
         load_scale_planes(nc, k_planes, Wk_scales)
-        cos_pairs, sin_planes = build_rope_tables(nc, consts)
 
         q_acc = [psum.tile([P, N_TILE], F32, tag="bank%d" % b, name="q_acc%d" % b) for b in range(BANKS)]
         for g in range(GROUPS):
@@ -204,9 +212,7 @@ def tile_multiheadselfattention_pa_k_kernel(
             for b in range(BANKS):
                 cols = slice(b * N_TILE, (b + 1) * N_TILE)
                 multiply(nc, q_acc[b], x_codes, x_scales, g, w_tile[:, cols], q_planes, cols)
-        for b in range(BANKS):
-            heads = slice(b * HEADS_PER_BANK, (b + 1) * HEADS_PER_BANK)
-            rotate_and_store(nc, work, q_acc[b], cos_pairs, sin_planes, out_0[0, heads], nc.scalar)
+        q_rotated = [rotate(nc, work, results, q_acc[b], cos_pairs, sin_planes) for b in range(BANKS)]
 
         k_acc = [
             psum.tile([P, N_TILE], F32, tag="bank%d" % (BANKS + b), name="k_acc%d" % b) for b in range(BANKS)
@@ -219,18 +225,22 @@ def tile_multiheadselfattention_pa_k_kernel(
             for b in range(BANKS):
                 cols = slice(b * N_TILE, (b + 1) * N_TILE)
                 multiply(nc, k_acc[b], x_codes, x_scales, g, w_tile[:, cols], k_planes, cols)
+        tail_tiles = []
         for b in range(BANKS):
-            cols = slice(b * N_TILE, (b + 1) * N_TILE)
             w_tile = weights.tile([P, TAIL_GROUPS, N_TILE], U32, tag="w", name="wk_tail", align_bytes=64)
             nc.sync.dma_start(
                 out=w_tile[:].bitcast(I32),
-                in_=Wk_words[GROUPS - TAIL_GROUPS : GROUPS, :, cols, :]
+                in_=Wk_words[GROUPS - TAIL_GROUPS : GROUPS, :, b * N_TILE : (b + 1) * N_TILE, :]
                 .rearrange("g p n t -> p g (n t)")
                 .bitcast(I32),
             )
+            tail_tiles.append(w_tile)
+
+        for b in range(BANKS):
+            store(nc, q_rotated[b], out_0, b)
+        for b in range(BANKS):
+            cols = slice(b * N_TILE, (b + 1) * N_TILE)
             for i in range(TAIL_GROUPS):
-                multiply(
-                    nc, k_acc[b], x_codes, x_scales, GROUPS - TAIL_GROUPS + i, w_tile[:, i, :], k_planes, cols
-                )
-            heads = slice(b * HEADS_PER_BANK, (b + 1) * HEADS_PER_BANK)
-            rotate_and_store(nc, work, k_acc[b], cos_pairs, sin_planes, out_1[0, heads], nc.sync)
+                g = GROUPS - TAIL_GROUPS + i
+                multiply(nc, k_acc[b], x_codes, x_scales, g, tail_tiles[b][:, i, :], k_planes, cols)
+            store(nc, rotate(nc, work, results, k_acc[b], cos_pairs, sin_planes), out_1, b)

@@ -30,7 +30,8 @@ PLANE_ROWS = 4
 PLANES_PER_SET = 4
 SETS = GROUPS // PLANES_PER_SET
 TAIL_GROUPS = 4
-W_BUFS = 12
+GROUPS_PER_LOAD = 2
+W_BUFS = 8
 
 FLOPS = 2 * P * FEATURES * 2 * N_OUT
 
@@ -134,6 +135,15 @@ def load_scale_planes(nc, planes, scales):
             )
 
 
+def load_groups(nc, weights, words, first):
+    w_tile = weights.tile([P, GROUPS_PER_LOAD, N_OUT], U32, tag="w", name="w_tile", align_bytes=64)
+    nc.sync.dma_start(
+        out=w_tile[:].bitcast(I32),
+        in_=words[first : first + GROUPS_PER_LOAD].rearrange("g p n t -> p g (n t)").bitcast(I32),
+    )
+    return w_tile
+
+
 def multiply(nc, acc, x_codes, x_scales, g, w_codes, planes, cols):
     positions = slice(g * P, (g + 1) * P)
     first_row = PLANE_ROWS * (g % PLANES_PER_SET)
@@ -204,27 +214,23 @@ def tile_multiheadselfattention_pa_k_kernel(
         load_scale_planes(nc, k_planes, Wk_scales)
 
         q_acc = [psum.tile([P, N_TILE], F32, tag="bank%d" % b, name="q_acc%d" % b) for b in range(BANKS)]
-        for g in range(GROUPS):
-            w_tile = weights.tile([P, N_OUT], U32, tag="w", name="wq", align_bytes=64)
-            nc.sync.dma_start(
-                out=w_tile[:].bitcast(I32), in_=Wq_words[g].rearrange("p n t -> p (n t)").bitcast(I32)
-            )
-            for b in range(BANKS):
-                cols = slice(b * N_TILE, (b + 1) * N_TILE)
-                multiply(nc, q_acc[b], x_codes, x_scales, g, w_tile[:, cols], q_planes, cols)
+        for first in range(0, GROUPS, GROUPS_PER_LOAD):
+            w_tile = load_groups(nc, weights, Wq_words, first)
+            for g in range(first, first + GROUPS_PER_LOAD):
+                for b in range(BANKS):
+                    cols = slice(b * N_TILE, (b + 1) * N_TILE)
+                    multiply(nc, q_acc[b], x_codes, x_scales, g, w_tile[:, g - first, cols], q_planes, cols)
         q_rotated = [rotate(nc, work, results, q_acc[b], cos_pairs, sin_planes) for b in range(BANKS)]
 
         k_acc = [
             psum.tile([P, N_TILE], F32, tag="bank%d" % (BANKS + b), name="k_acc%d" % b) for b in range(BANKS)
         ]
-        for g in range(GROUPS - TAIL_GROUPS):
-            w_tile = weights.tile([P, N_OUT], U32, tag="w", name="wk", align_bytes=64)
-            nc.sync.dma_start(
-                out=w_tile[:].bitcast(I32), in_=Wk_words[g].rearrange("p n t -> p (n t)").bitcast(I32)
-            )
-            for b in range(BANKS):
-                cols = slice(b * N_TILE, (b + 1) * N_TILE)
-                multiply(nc, k_acc[b], x_codes, x_scales, g, w_tile[:, cols], k_planes, cols)
+        for first in range(0, GROUPS - TAIL_GROUPS, GROUPS_PER_LOAD):
+            w_tile = load_groups(nc, weights, Wk_words, first)
+            for g in range(first, first + GROUPS_PER_LOAD):
+                for b in range(BANKS):
+                    cols = slice(b * N_TILE, (b + 1) * N_TILE)
+                    multiply(nc, k_acc[b], x_codes, x_scales, g, w_tile[:, g - first, cols], k_planes, cols)
         tail_tiles = []
         for b in range(BANKS):
             w_tile = weights.tile([P, TAIL_GROUPS, N_TILE], U32, tag="w", name="wk_tail", align_bytes=64)

@@ -23,12 +23,15 @@ N_OUT = HEADS * HEAD_DIM
 N_TILE = 512
 BANKS = N_OUT // N_TILE
 HEADS_PER_BANK = N_TILE // HEAD_DIM
+RUN = HEADS_PER_BANK
 ROPE_BASE = 10000.0
 ROUND_MAGIC = 1.5 * 2.0**23
 
 PLANE_ROWS = 4
 PLANES_PER_SET = 4
 SETS = GROUPS // PLANES_PER_SET
+FLIP_AFTER = 4
+RUNS_AFTER = 6
 TAIL_GROUPS = 4
 GROUPS_PER_LOAD = 2
 W_BUFS = 8
@@ -122,7 +125,7 @@ def quantise_x(nc, consts, psum, x):
                 scales=x_scales[:, first_pass * P : last_pass * P],
                 in_=grouped[:, first_pass * K_PASS : last_pass * K_PASS],
             )
-    return x_codes, x_scales
+    return x_codes, x_scales, identity
 
 
 def load_scale_planes(nc, planes, scales):
@@ -158,25 +161,25 @@ def multiply(nc, acc, x_codes, x_scales, g, w_codes, planes, cols):
     )
 
 
-def rotate(nc, work, results, acc, cos_pairs, sin_planes):
-    by_head = "p (h j) -> p h j"
-    pairs = acc[:].rearrange("p (h i e) -> p h i e", h=HEADS_PER_BANK, e=2)
-    half_shape = [P, HEADS_PER_BANK, HALF]
+def rotate(nc, work, results, acc, first_head, heads, cos_pairs, sin_planes):
+    width = heads * HEAD_DIM
+    t = acc[:, first_head * HEAD_DIM : first_head * HEAD_DIM + width]
+    pairs = t.rearrange("p (h i e) -> p h i e", h=heads, e=2)
 
-    direct = work.tile([P, N_TILE], F32)
+    direct = work.tile([P, width], F32)
     nc.vector.tensor_mul(
-        out=direct[:].rearrange(by_head, h=HEADS_PER_BANK),
-        in0=acc[:].rearrange(by_head, h=HEADS_PER_BANK),
-        in1=cos_pairs[:].rearrange("p i e -> p (i e)").unsqueeze(1).to_broadcast([P, HEADS_PER_BANK, HEAD_DIM]),
+        out=direct[:].rearrange("p (h j) -> p h j", h=heads),
+        in0=t.rearrange("p (h j) -> p h j", h=heads),
+        in1=cos_pairs[:].rearrange("p i e -> p (i e)").unsqueeze(1).to_broadcast([P, heads, HEAD_DIM]),
     )
-    cross = work.tile([P, 2, N_TILE // 2], F32)
+    cross = work.tile([P, 2, width // 2], F32)
     for e in range(2):
         nc.vector.tensor_mul(
-            out=cross[:, e, :].rearrange("p (h i) -> p h i", h=HEADS_PER_BANK),
+            out=cross[:, e, :].rearrange("p (h i) -> p h i", h=heads),
             in0=pairs[:, :, :, 1 - e],
-            in1=sin_planes[:, e, :].unsqueeze(1).to_broadcast(half_shape),
+            in1=sin_planes[:, e, :].unsqueeze(1).to_broadcast([P, heads, HALF]),
         )
-    rotated = results.tile([P, N_TILE], F32)
+    rotated = results.tile([P, width], F32)
     nc.vector.tensor_add(
         out=rotated[:].rearrange("p (n e) -> p n e", e=2),
         in0=direct[:].rearrange("p (n e) -> p n e", e=2),
@@ -185,12 +188,40 @@ def rotate(nc, work, results, acc, cos_pairs, sin_planes):
     return rotated
 
 
-def store(nc, rotated, out, b):
-    heads = slice(b * HEADS_PER_BANK, (b + 1) * HEADS_PER_BANK)
+def heads_first(nc, shuffle, psum, rotated, identity):
+    flipped = []
+    for b in range(BANKS):
+        turned = psum.tile([P, HEADS_PER_BANK, P], F32, tag="bank%d" % b, name="turned")
+        for h in range(HEADS_PER_BANK):
+            nc.tensor.transpose(turned[:, h, :], rotated[b][:, h * HEAD_DIM : (h + 1) * HEAD_DIM], identity[:])
+        flip = shuffle.tile([P, N_TILE], F32)
+        nc.scalar.copy(out=flip[:], in_=turned[:].rearrange("p h r -> p (h r)"))
+        flipped.append(flip)
+    return flipped
+
+
+def positions_in_runs(nc, shuffle, psum, flipped, identity):
+    in_runs = []
+    for b in range(BANKS):
+        turned = psum.tile([P, RUN, HEAD_DIM], F32, tag="bank%d" % b, name="turned_back")
+        for c in range(RUN):
+            nc.tensor.transpose(turned[:, c, :], flipped[b][:, c::RUN], identity[:])
+        runs = shuffle.tile([P, N_TILE], F32)
+        nc.scalar.copy(out=runs[:], in_=turned[:].rearrange("p c j -> p (c j)"))
+        in_runs.append(runs)
+    return in_runs
+
+
+def store(nc, rotated, out, first_head, heads):
     nc.sync.dma_start(
-        out=out[0, heads].rearrange("h p j -> p h j"),
-        in_=rotated[:].rearrange("p (h j) -> p h j", h=HEADS_PER_BANK),
+        out=out[0, first_head : first_head + heads].rearrange("h p j -> p h j"),
+        in_=rotated[:].rearrange("p (h j) -> p h j", h=heads),
     )
+
+
+def store_runs(nc, runs, out, b):
+    heads = slice(b * HEADS_PER_BANK, (b + 1) * HEADS_PER_BANK)
+    nc.sync.dma_start(out=out[0, heads].rearrange("h (q c) j -> (h q) (c j)", c=RUN), in_=runs[:])
 
 
 def tile_multiheadselfattention_pa_k_kernel(
@@ -200,8 +231,8 @@ def tile_multiheadselfattention_pa_k_kernel(
     with tc.tile_pool(name="consts", bufs=1) as consts, tc.tile_pool(
         name="weights", bufs=W_BUFS
     ) as weights, tc.tile_pool(name="work", bufs=2) as work, tc.tile_pool(
-        name="results", bufs=2 * BANKS
-    ) as results, tc.psum_pool(name="psum", bufs=1) as psum, tc.manual_schedule():
+        name="results", bufs=2 * BANKS + 1
+    ) as results, tc.tile_pool(name="shuffle", bufs=BANKS) as shuffle, tc.psum_pool(name="psum", bufs=1) as psum, tc.manual_schedule():
 
         q_planes = consts.tile([P, SETS, N_OUT], U8, align_bytes=64)
         k_planes = consts.tile([P, SETS, N_OUT], U8, align_bytes=64)
@@ -209,7 +240,7 @@ def tile_multiheadselfattention_pa_k_kernel(
         nc.vector.memset(k_planes[:].bitcast(I32), 0)
 
         cos_pairs, sin_planes = build_rope_tables(nc, consts)
-        x_codes, x_scales = quantise_x(nc, consts, psum, x)
+        x_codes, x_scales, identity = quantise_x(nc, consts, psum, x)
         load_scale_planes(nc, q_planes, Wq_scales)
         load_scale_planes(nc, k_planes, Wk_scales)
 
@@ -220,7 +251,9 @@ def tile_multiheadselfattention_pa_k_kernel(
                 for b in range(BANKS):
                     cols = slice(b * N_TILE, (b + 1) * N_TILE)
                     multiply(nc, q_acc[b], x_codes, x_scales, g, w_tile[:, g - first, cols], q_planes, cols)
-        q_rotated = [rotate(nc, work, results, q_acc[b], cos_pairs, sin_planes) for b in range(BANKS)]
+        q_rotated = [
+            rotate(nc, work, results, q_acc[b], 0, HEADS_PER_BANK, cos_pairs, sin_planes) for b in range(BANKS)
+        ]
 
         k_acc = [
             psum.tile([P, N_TILE], F32, tag="bank%d" % (BANKS + b), name="k_acc%d" % b) for b in range(BANKS)
@@ -231,22 +264,32 @@ def tile_multiheadselfattention_pa_k_kernel(
                 for b in range(BANKS):
                     cols = slice(b * N_TILE, (b + 1) * N_TILE)
                     multiply(nc, k_acc[b], x_codes, x_scales, g, w_tile[:, g - first, cols], k_planes, cols)
+            if first == FLIP_AFTER:
+                q_flipped = heads_first(nc, shuffle, psum, q_rotated, identity)
+            if first == RUNS_AFTER:
+                q_runs = positions_in_runs(nc, shuffle, psum, q_flipped, identity)
         tail_tiles = []
         for b in range(BANKS):
             w_tile = weights.tile([P, TAIL_GROUPS, N_TILE], U32, tag="w", name="wk_tail", align_bytes=64)
-            nc.sync.dma_start(
-                out=w_tile[:].bitcast(I32),
-                in_=Wk_words[GROUPS - TAIL_GROUPS : GROUPS, :, b * N_TILE : (b + 1) * N_TILE, :]
-                .rearrange("g p n t -> p g (n t)")
-                .bitcast(I32),
-            )
+            step = TAIL_GROUPS if b < BANKS - 1 else 1
+            for i in range(0, TAIL_GROUPS, step):
+                g = GROUPS - TAIL_GROUPS + i
+                nc.sync.dma_start(
+                    out=w_tile[:, i : i + step, :].bitcast(I32),
+                    in_=Wk_words[g : g + step, :, b * N_TILE : (b + 1) * N_TILE, :]
+                    .rearrange("g p n t -> p g (n t)")
+                    .bitcast(I32),
+                )
             tail_tiles.append(w_tile)
 
         for b in range(BANKS):
-            store(nc, q_rotated[b], out_0, b)
+            store_runs(nc, q_runs[b], out_0, b)
         for b in range(BANKS):
             cols = slice(b * N_TILE, (b + 1) * N_TILE)
             for i in range(TAIL_GROUPS):
                 g = GROUPS - TAIL_GROUPS + i
                 multiply(nc, k_acc[b], x_codes, x_scales, g, tail_tiles[b][:, i, :], k_planes, cols)
-            store(nc, rotate(nc, work, results, k_acc[b], cos_pairs, sin_planes), out_1, b)
+            heads = HEADS_PER_BANK if b < BANKS - 1 else HEADS_PER_BANK // 2
+            for first_head in range(0, HEADS_PER_BANK, heads):
+                rotated = rotate(nc, work, results, k_acc[b], first_head, heads, cos_pairs, sin_planes)
+                store(nc, rotated, out_1, b * HEADS_PER_BANK + first_head, heads)

@@ -32,7 +32,11 @@ PLANES_PER_SET = 4
 SETS = GROUPS // PLANES_PER_SET
 FLIP_AFTER = 4
 RUNS_AFTER = 6
-TAIL_GROUPS = 4
+TAIL_GROUPS = 6
+LAST_GROUPS = 2
+K_PIECES = [(0, N_TILE), (N_TILE, N_TILE), (2 * N_TILE, N_TILE), (3 * N_TILE, N_TILE // 2), (7 * N_TILE // 2, N_TILE // 2)]
+K_BANKS = [4, 5, 6, 7, 0]
+SHUFFLE_BANKS = [1, 2, 3, 1]
 GROUPS_PER_LOAD = 2
 W_BUFS = 8
 
@@ -161,9 +165,9 @@ def multiply(nc, acc, x_codes, x_scales, g, w_codes, planes, cols):
     )
 
 
-def rotate(nc, work, results, acc, first_head, heads, cos_pairs, sin_planes):
-    width = heads * HEAD_DIM
-    t = acc[:, first_head * HEAD_DIM : first_head * HEAD_DIM + width]
+def rotate(nc, work, results, acc, width, cos_pairs, sin_planes):
+    heads = width // HEAD_DIM
+    t = acc[:]
     pairs = t.rearrange("p (h i e) -> p h i e", h=heads, e=2)
 
     direct = work.tile([P, width], F32)
@@ -191,7 +195,7 @@ def rotate(nc, work, results, acc, first_head, heads, cos_pairs, sin_planes):
 def heads_first(nc, shuffle, psum, rotated, identity):
     flipped = []
     for b in range(BANKS):
-        turned = psum.tile([P, HEADS_PER_BANK, P], F32, tag="bank%d" % b, name="turned")
+        turned = psum.tile([P, HEADS_PER_BANK, P], F32, tag="bank%d" % SHUFFLE_BANKS[b], name="turned")
         for h in range(HEADS_PER_BANK):
             nc.tensor.transpose(turned[:, h, :], rotated[b][:, h * HEAD_DIM : (h + 1) * HEAD_DIM], identity[:])
         flip = shuffle.tile([P, N_TILE], F32)
@@ -203,7 +207,7 @@ def heads_first(nc, shuffle, psum, rotated, identity):
 def positions_in_runs(nc, shuffle, psum, flipped, identity):
     in_runs = []
     for b in range(BANKS):
-        turned = psum.tile([P, RUN, HEAD_DIM], F32, tag="bank%d" % b, name="turned_back")
+        turned = psum.tile([P, RUN, HEAD_DIM], F32, tag="bank%d" % SHUFFLE_BANKS[b], name="turned_back")
         for c in range(RUN):
             nc.tensor.transpose(turned[:, c, :], flipped[b][:, c::RUN], identity[:])
         runs = shuffle.tile([P, N_TILE], F32)
@@ -252,44 +256,44 @@ def tile_multiheadselfattention_pa_k_kernel(
                     cols = slice(b * N_TILE, (b + 1) * N_TILE)
                     multiply(nc, q_acc[b], x_codes, x_scales, g, w_tile[:, g - first, cols], q_planes, cols)
         q_rotated = [
-            rotate(nc, work, results, q_acc[b], 0, HEADS_PER_BANK, cos_pairs, sin_planes) for b in range(BANKS)
+            rotate(nc, work, results, q_acc[b], N_TILE, cos_pairs, sin_planes) for b in range(BANKS)
         ]
 
         k_acc = [
-            psum.tile([P, N_TILE], F32, tag="bank%d" % (BANKS + b), name="k_acc%d" % b) for b in range(BANKS)
+            psum.tile([P, width], F32, tag="bank%d" % bank, name="k_acc%d" % bank)
+            for bank, (start, width) in zip(K_BANKS, K_PIECES)
         ]
         for first in range(0, GROUPS - TAIL_GROUPS, GROUPS_PER_LOAD):
             w_tile = load_groups(nc, weights, Wk_words, first)
             for g in range(first, first + GROUPS_PER_LOAD):
-                for b in range(BANKS):
-                    cols = slice(b * N_TILE, (b + 1) * N_TILE)
-                    multiply(nc, k_acc[b], x_codes, x_scales, g, w_tile[:, g - first, cols], k_planes, cols)
+                for acc, (start, width) in zip(k_acc, K_PIECES):
+                    cols = slice(start, start + width)
+                    multiply(nc, acc, x_codes, x_scales, g, w_tile[:, g - first, cols], k_planes, cols)
             if first == FLIP_AFTER:
                 q_flipped = heads_first(nc, shuffle, psum, q_rotated, identity)
             if first == RUNS_AFTER:
                 q_runs = positions_in_runs(nc, shuffle, psum, q_flipped, identity)
         tail_tiles = []
-        for b in range(BANKS):
-            w_tile = weights.tile([P, TAIL_GROUPS, N_TILE], U32, tag="w", name="wk_tail", align_bytes=64)
-            step = TAIL_GROUPS if b < BANKS - 1 else 1
-            for i in range(0, TAIL_GROUPS, step):
-                g = GROUPS - TAIL_GROUPS + i
-                nc.sync.dma_start(
-                    out=w_tile[:, i : i + step, :].bitcast(I32),
-                    in_=Wk_words[g : g + step, :, b * N_TILE : (b + 1) * N_TILE, :]
-                    .rearrange("g p n t -> p g (n t)")
-                    .bitcast(I32),
-                )
+        for start, width in K_PIECES:
+            w_tile = weights.tile([P, TAIL_GROUPS, width], U32, tag="w", name="wk_tail", align_bytes=64)
+            first_part = TAIL_GROUPS if start + width < N_OUT else TAIL_GROUPS - LAST_GROUPS
+            for i0, i1 in [(0, first_part), (first_part, TAIL_GROUPS)]:
+                if i0 < i1:
+                    g = GROUPS - TAIL_GROUPS
+                    nc.sync.dma_start(
+                        out=w_tile[:, i0:i1, :].bitcast(I32),
+                        in_=Wk_words[g + i0 : g + i1, :, start : start + width, :]
+                        .rearrange("g p n t -> p g (n t)")
+                        .bitcast(I32),
+                    )
             tail_tiles.append(w_tile)
 
         for b in range(BANKS):
             store_runs(nc, q_runs[b], out_0, b)
-        for b in range(BANKS):
-            cols = slice(b * N_TILE, (b + 1) * N_TILE)
+        for acc, w_tile, (start, width) in zip(k_acc, tail_tiles, K_PIECES):
+            cols = slice(start, start + width)
             for i in range(TAIL_GROUPS):
                 g = GROUPS - TAIL_GROUPS + i
-                multiply(nc, k_acc[b], x_codes, x_scales, g, tail_tiles[b][:, i, :], k_planes, cols)
-            heads = HEADS_PER_BANK if b < BANKS - 1 else HEADS_PER_BANK // 2
-            for first_head in range(0, HEADS_PER_BANK, heads):
-                rotated = rotate(nc, work, results, k_acc[b], first_head, heads, cos_pairs, sin_planes)
-                store(nc, rotated, out_1, b * HEADS_PER_BANK + first_head, heads)
+                multiply(nc, acc, x_codes, x_scales, g, w_tile[:, i, :], k_planes, cols)
+            rotated = rotate(nc, work, results, acc, width, cos_pairs, sin_planes)
+            store(nc, rotated, out_1, start // HEAD_DIM, width // HEAD_DIM)

import math

import concourse.mybir as mybir
from concourse.masks import make_identity

F32 = mybir.dt.float32
BF16 = mybir.dt.bfloat16
I32 = mybir.dt.int32
U32 = mybir.dt.uint32
U8 = mybir.dt.uint8
FP8X4 = mybir.dt.float8_e4m3fn_x4
SIN = mybir.ActivationFunctionType.Sin

P = 128
PACK = 4
K_PASS = P * PACK
FEATURES = 8192
GROUPS = FEATURES // K_PASS
HEADS = 16
HEAD_DIM = 128
HALF = HEAD_DIM // 2
N_OUT = HEADS * HEAD_DIM
N_TILE = 512
BANKS = N_OUT // N_TILE
HEADS_PER_BANK = N_TILE // HEAD_DIM
RUN = HEADS_PER_BANK
ROPE_BASE = 10000.0
ROUND_MAGIC = 1.5 * 2.0**23

PLANE_ROWS = 4
PLANES_PER_SET = 4
SETS = GROUPS // PLANES_PER_SET
FLIP_AFTER = 4
RUNS_AFTER = 6
TAIL_GROUPS = 6
LAST_GROUPS = 2
K_PIECES = [(0, N_TILE), (N_TILE, N_TILE), (2 * N_TILE, N_TILE), (3 * N_TILE, N_TILE // 2), (7 * N_TILE // 2, N_TILE // 2)]
K_BANKS = [4, 5, 6, 7, 0]
SHUFFLE_BANKS = [1, 2, 3, 1]
GROUPS_PER_LOAD = 2
W_BUFS = 8

FLOPS = 2 * P * FEATURES * 2 * N_OUT


def build_rope_tables(nc, consts):
    position_int = consts.tile([P, 1], I32)
    nc.gpsimd.iota(position_int[:], pattern=[[0, 1]], base=0, channel_multiplier=1)
    position = consts.tile([P, 1], F32)
    nc.vector.tensor_copy(out=position[:], in_=position_int[:])
    position_turns = consts.tile([P, 1], F32)
    nc.vector.tensor_scalar_mul(out=position_turns[:], in0=position[:], scalar1=1.0 / (2.0 * math.pi))

    frequency = consts.tile([P, HALF], F32)
    nc.vector.memset(frequency[:, 0:1], 1.0)
    width = 1
    while width < HALF:
        nc.vector.tensor_scalar_mul(
            out=frequency[:, width : 2 * width],
            in0=frequency[:, 0:width],
            scalar1=ROPE_BASE ** (-2.0 * width / HEAD_DIM),
        )
        width *= 2

    turns = consts.tile([P, 2, HALF], F32)
    nc.vector.tensor_scalar_mul(out=turns[:, 0, :], in0=frequency[:], scalar1=position_turns[:, 0:1])
    nc.vector.tensor_scalar_add(out=turns[:, 1, :], in0=turns[:, 0, :], scalar1=0.25)

    shifted = consts.tile([P, 2, HALF], F32)
    nc.vector.tensor_scalar_add(out=shifted[:], in0=turns[:], scalar1=ROUND_MAGIC)
    whole = consts.tile([P, 2, HALF], F32)
    nc.vector.tensor_scalar_sub(out=whole[:], in0=shifted[:], scalar1=ROUND_MAGIC)
    part = consts.tile([P, 2, HALF], F32)
    nc.vector.tensor_sub(out=part[:], in0=turns[:], in1=whole[:])

    cos_pairs = consts.tile([P, HALF, 2], F32)
    nc.scalar.activation(
        out=cos_pairs[:],
        in_=part[:, 1, :].unsqueeze(2).to_broadcast([P, HALF, 2]),
        func=SIN,
        scale=2.0 * math.pi,
    )
    sin_planes = consts.tile([P, 2, HALF], F32)
    nc.scalar.activation(out=sin_planes[:, 0, :], in_=part[:, 0, :], func=SIN, scale=-2.0 * math.pi)
    nc.scalar.activation(out=sin_planes[:, 1, :], in_=part[:, 0, :], func=SIN, scale=2.0 * math.pi)
    return cos_pairs, sin_planes


def quantise_x(nc, consts, psum, x):
    identity = consts.tile([P, P], F32)
    make_identity(nc, identity[:])

    x_sb = consts.tile([P, FEATURES], BF16)
    load_cols = FEATURES // 4
    for piece in range(4):
        cols = slice(piece * load_cols, (piece + 1) * load_cols)
        nc.sync.dma_start(out=x_sb[:, cols], in_=x[0, :, cols])

    x_words = x_sb[:].bitcast(F32)
    words_per_pass = K_PASS // 2
    grouped = consts.tile([P, GROUPS * K_PASS], BF16, align_bytes=64)
    grouped_words = grouped[:].bitcast(F32)
    x_codes = consts.tile([P, GROUPS * P], U32, align_bytes=64)
    x_scales = consts.tile([P, GROUPS * P], U8, align_bytes=64)

    passes_per_bank = 2
    banks_per_quantise = 2
    for bank in range(GROUPS // passes_per_bank):
        xt = psum.tile([P, 2 * passes_per_bank, P], F32, tag="bank%d" % bank, name="xt")
        for c in range(passes_per_bank):
            first_word = (bank * passes_per_bank + c) * words_per_pass
            for u in range(2):
                nc.tensor.transpose(
                    xt[:, 2 * c + u, :],
                    x_words[:, first_word + u : first_word + words_per_pass : 2],
                    identity[:],
                )
        bank_words = slice(bank * N_TILE, (bank + 1) * N_TILE)
        side_by_side = grouped_words[:, bank_words].rearrange("p (c r u) -> p c r u", c=passes_per_bank, u=2)
        transposed = xt[:].rearrange("p (c u) r -> p c r u", u=2)
        if bank % 2 == 0:
            nc.vector.tensor_copy(out=side_by_side, in_=transposed)
        else:
            nc.scalar.copy(out=side_by_side, in_=transposed)
            first_pass = (bank + 1 - banks_per_quantise) * passes_per_bank
            last_pass = (bank + 1) * passes_per_bank
            nc.vector.quantize_mx(
                out=x_codes[:, first_pass * P : last_pass * P].bitcast(FP8X4),
                scales=x_scales[:, first_pass * P : last_pass * P],
                in_=grouped[:, first_pass * K_PASS : last_pass * K_PASS],
            )
    return x_codes, x_scales, identity


def load_scale_planes(nc, planes, scales):
    for s in range(SETS):
        groups = slice(s * PLANES_PER_SET, (s + 1) * PLANES_PER_SET)
        for quadrant in range(4):
            nc.gpsimd.dma_start(
                out=planes[32 * quadrant : 32 * quadrant + PLANES_PER_SET * PLANE_ROWS, s, :].bitcast(F32),
                in_=scales[groups, PLANE_ROWS * quadrant : PLANE_ROWS * (quadrant + 1), :].bitcast(F32),
            )


def load_groups(nc, weights, words, first):
    w_tile = weights.tile([P, GROUPS_PER_LOAD, N_OUT], U32, tag="w", name="w_tile", align_bytes=64)
    nc.sync.dma_start(
        out=w_tile[:].bitcast(I32),
        in_=words[first : first + GROUPS_PER_LOAD].rearrange("g p n t -> p g (n t)").bitcast(I32),
    )
    return w_tile


def multiply(nc, acc, x_codes, x_scales, g, w_codes, planes, cols):
    positions = slice(g * P, (g + 1) * P)
    first_row = PLANE_ROWS * (g % PLANES_PER_SET)
    nc.tensor.matmul_mx(
        out=acc[:],
        lhsT=x_codes[:, positions].bitcast(FP8X4),
        lhsT_scale=x_scales[:, positions],
        rhs=w_codes.bitcast(FP8X4),
        rhs_scale=planes[first_row:P, g // PLANES_PER_SET, cols],
        start=(g == 0),
        stop=(g == GROUPS - 1),
    )


def rotate(nc, work, results, acc, width, cos_pairs, sin_planes):
    heads = width // HEAD_DIM
    t = acc[:]
    pairs = t.rearrange("p (h i e) -> p h i e", h=heads, e=2)

    direct = work.tile([P, width], F32)
    nc.vector.tensor_mul(
        out=direct[:].rearrange("p (h j) -> p h j", h=heads),
        in0=t.rearrange("p (h j) -> p h j", h=heads),
        in1=cos_pairs[:].rearrange("p i e -> p (i e)").unsqueeze(1).to_broadcast([P, heads, HEAD_DIM]),
    )
    cross = work.tile([P, 2, width // 2], F32)
    for e in range(2):
        nc.vector.tensor_mul(
            out=cross[:, e, :].rearrange("p (h i) -> p h i", h=heads),
            in0=pairs[:, :, :, 1 - e],
            in1=sin_planes[:, e, :].unsqueeze(1).to_broadcast([P, heads, HALF]),
        )
    rotated = results.tile([P, width], F32)
    nc.vector.tensor_add(
        out=rotated[:].rearrange("p (n e) -> p n e", e=2),
        in0=direct[:].rearrange("p (n e) -> p n e", e=2),
        in1=cross[:].rearrange("p e n -> p n e"),
    )
    return rotated


def heads_first(nc, shuffle, psum, rotated, identity):
    flipped = []
    for b in range(BANKS):
        turned = psum.tile([P, HEADS_PER_BANK, P], F32, tag="bank%d" % SHUFFLE_BANKS[b], name="turned")
        for h in range(HEADS_PER_BANK):
            nc.tensor.transpose(turned[:, h, :], rotated[b][:, h * HEAD_DIM : (h + 1) * HEAD_DIM], identity[:])
        flip = shuffle.tile([P, N_TILE], F32)
        nc.scalar.copy(out=flip[:], in_=turned[:].rearrange("p h r -> p (h r)"))
        flipped.append(flip)
    return flipped


def positions_in_runs(nc, shuffle, psum, flipped, identity):
    in_runs = []
    for b in range(BANKS):
        turned = psum.tile([P, RUN, HEAD_DIM], F32, tag="bank%d" % SHUFFLE_BANKS[b], name="turned_back")
        for c in range(RUN):
            nc.tensor.transpose(turned[:, c, :], flipped[b][:, c::RUN], identity[:])
        runs = shuffle.tile([P, N_TILE], F32)
        nc.scalar.copy(out=runs[:], in_=turned[:].rearrange("p c j -> p (c j)"))
        in_runs.append(runs)
    return in_runs


def store(nc, rotated, out, first_head, heads):
    nc.sync.dma_start(
        out=out[0, first_head : first_head + heads].rearrange("h p j -> p h j"),
        in_=rotated[:].rearrange("p (h j) -> p h j", h=heads),
    )


def store_runs(nc, runs, out, b):
    heads = slice(b * HEADS_PER_BANK, (b + 1) * HEADS_PER_BANK)
    nc.sync.dma_start(out=out[0, heads].rearrange("h (q c) j -> (h q) (c j)", c=RUN), in_=runs[:])


def tile_multiheadselfattention_pa_k_kernel(
    tc, x, Wq_words, Wq_scales, Wk_words, Wk_scales, out_0, out_1
):
    nc = tc.nc
    with tc.tile_pool(name="consts", bufs=1) as consts, tc.tile_pool(
        name="weights", bufs=W_BUFS
    ) as weights, tc.tile_pool(name="work", bufs=2) as work, tc.tile_pool(
        name="results", bufs=2 * BANKS + 1
    ) as results, tc.tile_pool(name="shuffle", bufs=BANKS) as shuffle, tc.psum_pool(name="psum", bufs=1) as psum, tc.manual_schedule():

        q_planes = consts.tile([P, SETS, N_OUT], U8, align_bytes=64)
        k_planes = consts.tile([P, SETS, N_OUT], U8, align_bytes=64)
        nc.vector.memset(q_planes[:].bitcast(I32), 0)
        nc.vector.memset(k_planes[:].bitcast(I32), 0)

        cos_pairs, sin_planes = build_rope_tables(nc, consts)
        x_codes, x_scales, identity = quantise_x(nc, consts, psum, x)
        load_scale_planes(nc, q_planes, Wq_scales)
        load_scale_planes(nc, k_planes, Wk_scales)

        q_acc = [psum.tile([P, N_TILE], F32, tag="bank%d" % b, name="q_acc%d" % b) for b in range(BANKS)]
        for first in range(0, GROUPS, GROUPS_PER_LOAD):
            w_tile = load_groups(nc, weights, Wq_words, first)
            for g in range(first, first + GROUPS_PER_LOAD):
                for b in range(BANKS):
                    cols = slice(b * N_TILE, (b + 1) * N_TILE)
                    multiply(nc, q_acc[b], x_codes, x_scales, g, w_tile[:, g - first, cols], q_planes, cols)
        q_rotated = [
            rotate(nc, work, results, q_acc[b], N_TILE, cos_pairs, sin_planes) for b in range(BANKS)
        ]

        k_acc = [
            psum.tile([P, width], F32, tag="bank%d" % bank, name="k_acc%d" % bank)
            for bank, (start, width) in zip(K_BANKS, K_PIECES)
        ]
        for first in range(0, GROUPS - TAIL_GROUPS, GROUPS_PER_LOAD):
            w_tile = load_groups(nc, weights, Wk_words, first)
            for g in range(first, first + GROUPS_PER_LOAD):
                for acc, (start, width) in zip(k_acc, K_PIECES):
                    cols = slice(start, start + width)
                    multiply(nc, acc, x_codes, x_scales, g, w_tile[:, g - first, cols], k_planes, cols)
            if first == FLIP_AFTER:
                q_flipped = heads_first(nc, shuffle, psum, q_rotated, identity)
            if first == RUNS_AFTER:
                q_runs = positions_in_runs(nc, shuffle, psum, q_flipped, identity)
        tail_tiles = []
        for start, width in K_PIECES:
            w_tile = weights.tile([P, TAIL_GROUPS, width], U32, tag="w", name="wk_tail", align_bytes=64)
            first_part = TAIL_GROUPS if start + width < N_OUT else TAIL_GROUPS - LAST_GROUPS
            for i0, i1 in [(0, first_part), (first_part, TAIL_GROUPS)]:
                if i0 < i1:
                    g = GROUPS - TAIL_GROUPS
                    nc.sync.dma_start(
                        out=w_tile[:, i0:i1, :].bitcast(I32),
                        in_=Wk_words[g + i0 : g + i1, :, start : start + width, :]
                        .rearrange("g p n t -> p g (n t)")
                        .bitcast(I32),
                    )
            tail_tiles.append(w_tile)

        for b in range(BANKS):
            store_runs(nc, q_runs[b], out_0, b)
        for acc, w_tile, (start, width) in zip(k_acc, tail_tiles, K_PIECES):
            cols = slice(start, start + width)
            for i in range(TAIL_GROUPS):
                g = GROUPS - TAIL_GROUPS + i
                multiply(nc, acc, x_codes, x_scales, g, w_tile[:, i, :], k_planes, cols)
            rotated = rotate(nc, work, results, acc, width, cos_pairs, sin_planes)
            store(nc, rotated, out_1, start // HEAD_DIM, width // HEAD_DIM)
